import numpy as np
import ml_dtypes


def mxq(x, axis, fmt="e4m3"):
    dtype, down = {"e4m3": (ml_dtypes.float8_e4m3fn, 7), "e5m2": (ml_dtypes.float8_e5m2, 14)}[fmt]
    v = np.moveaxis(np.asarray(x, np.float32).astype(ml_dtypes.bfloat16).astype(np.float64), axis, -1)
    blocks = v.reshape(v.shape[:-1] + (-1, 32))
    amax = np.abs(blocks).max(-1, keepdims=True)
    byte = np.maximum(np.where(amax > 0, np.frexp(amax)[1] - 1 + 127, 0) - down, 1)
    scale = np.exp2(byte - 127.0)
    codes = (blocks / scale).astype(np.float32).astype(dtype).astype(np.float64)
    return np.moveaxis((codes * scale).reshape(v.shape), -1, axis)


WIDE = False


def mx_kscale(k):
    if not WIDE:
        return np.ones(k)
    levels = np.array([10, -10, 5, -5, 0])
    a = np.random.permutation(np.resize(levels, k // 512 * 4)).reshape(k // 512, 4)
    idx = np.arange(k)
    return np.exp2(a[idx // 512, idx % 128 // 32])


BF16 = ml_dtypes.bfloat16


def bf(x):
    return np.asarray(x, np.float32).astype(BF16)


def f64(x):
    return np.asarray(x).astype(np.float64)


N, D, H, E = 256, 512, 8192, 2

CLAMP_MAX = float(np.log(100.0))


def setup_inputs():
    s, t = mx_kscale(D), mx_kscale(H)
    return {"x": bf(np.random.standard_normal((N, D)) * s),
            "W1": bf(np.random.standard_normal((E, D, H)) / np.sqrt(D) / s[:, None] * t),
            "b1": bf(np.random.standard_normal((E, H)) * 0.1 * t),
            "W2": bf(np.random.standard_normal((E, H, D)) / np.sqrt(H) / t[:, None]),
            "b2": bf(np.random.standard_normal((E, D)) * 0.1),
            "temperature": bf(np.log(2.0) + 0.1 * np.random.standard_normal((1,)))}


def reference(x, W1, b1, W2, b2, temperature):
    xe = f64(x).reshape(E, N // E, D)
    h = np.maximum((mxq(xe, 2, "e4m3") @ mxq(f64(W1), 1, "e4m3")) + f64(b1)[:, None, :], 0.0)
    y = (mxq(h, 2, "e4m3") @ mxq(f64(W2), 1, "e4m3")) + f64(b2)[:, None, :]
    logit_scale = np.exp(np.minimum(f64(temperature), CLAMP_MAX))
    return y.reshape(N, D) * logit_scale

@@ -1,0 +1,235 @@
+import math
+from contextlib import ExitStack
+
+import concourse.mybir as mybir
+from concourse.masks import make_identity
+
+BF16 = mybir.dt.bfloat16
+F32 = mybir.dt.float32
+U32 = mybir.dt.uint32
+U8 = mybir.dt.uint8
+FP8X4 = mybir.dt.float8_e4m3fn_x4
+ALU = mybir.AluOpType
+ACT = mybir.ActivationFunctionType
+
+P = 128
+PACK = 4
+K_PASS = P * PACK
+
+E = 2
+TOKENS = 128
+D = 512
+H = 8192
+
+CHUNK = 2048
+PASSES = CHUNK // D
+PAIRS = H // CHUNK
+N_CHUNKS = E * PAIRS * 2
+LOAD_AHEAD = 3
+B2_LOAD_STEP = LOAD_AHEAD
+B2_SCALE_STEP = 2 * LOAD_AHEAD
+
+HALF = CHUNK // 2
+VECTOR_WORDS = 384
+
+CLAMP_MAX = math.log(100.0)
+
+FLOPS = 2 * (2 * E * TOKENS * D * H)
+
+
+def tile_moelayer_k_kernel(tc, x, W1, b1, W2, b2, temperature, out):
+    nc = tc.nc
+    with ExitStack() as stack:
+        stack.enter_context(nc.allow_non_contiguous_dma(reason="temperature: one element a partition"))
+        const = stack.enter_context(tc.tile_pool(name="const", bufs=1))
+        raw_pool = stack.enter_context(tc.tile_pool(name="raw", bufs=LOAD_AHEAD + 1))
+        grouped_pool = stack.enter_context(tc.tile_pool(name="grouped", bufs=3))
+        operand_pool = stack.enter_context(tc.tile_pool(name="operand", bufs=3))
+        hidden_pool = stack.enter_context(tc.tile_pool(name="hidden", bufs=2))
+        psum_setup = stack.enter_context(tc.psum_pool(name="psum_setup", bufs=1))
+        psum_hidden = stack.enter_context(tc.psum_pool(name="psum_hidden", bufs=PASSES))
+        psum_y = stack.enter_context(tc.psum_pool(name="psum_y", bufs=E))
+
+        def place(u):
+            return u // (2 * PAIRS), (u // 2) % PAIRS, u % 2 == 1
+
+        def load_chunk(u):
+            e, c, is_w2 = place(u)
+            raw = raw_pool.tile([P, PACK, CHUNK], BF16, name="raw")
+            if not is_w2:
+                columns = W1[e, :, c * CHUNK : (c + 1) * CHUNK]
+                nc.sync.dma_start(out=raw[:], in_=columns.rearrange("(t p) w -> p t w", p=P))
+            else:
+                for q in range(PASSES):
+                    first_row = c * CHUNK + q * K_PASS
+                    rows = W2[e, first_row : first_row + K_PASS, :]
+                    nc.sync.dma_start(
+                        out=raw[:, :, q * D : (q + 1) * D],
+                        in_=rows.rearrange("(t p) d -> p t d", p=P),
+                    )
+            return raw
+
+        def regroup(raw):
+            grouped = grouped_pool.tile([P, CHUNK, PACK], BF16, name="grouped", align_bytes=64)
+
+            def views(first, last):
+                return (
+                    grouped[:, first:last, :].rearrange("p (c i) t -> p c t i", i=4),
+                    raw[:, :, first:last].rearrange("p t (c i) -> p c t i", i=4),
+                )
+
+            for half in range(0, CHUNK, HALF):
+                to, frm = views(half, half + VECTOR_WORDS)
+                nc.vector.tensor_copy(out=to, in_=frm)
+                to, frm = views(half + VECTOR_WORDS, half + HALF)
+                nc.scalar.copy(out=to, in_=frm)
+            return grouped
+
+        def quantise(grouped):
+            words = operand_pool.tile([P, CHUNK], U32, name="words", align_bytes=64)
+            scales = operand_pool.tile([P, CHUNK], U8, name="scales", align_bytes=64)
+            for half in range(0, CHUNK, HALF):
+                nc.vector.quantize_mx(
+                    out=words[:, half : half + HALF].bitcast(FP8X4),
+                    scales=scales[:, half : half + HALF],
+                    in_=grouped[:, half : half + HALF, :].rearrange("p w t -> p (w t)"),
+                )
+            return words, scales
+
+        x_rows = const.tile([P, E, D], BF16)
+        nc.scalar.dma_start(out=x_rows[:], in_=x.rearrange("(e n) k -> n e k", e=E))
+        b1_rows = const.tile([P, P], BF16)
+        nc.scalar.dma_start(out=b1_rows[:], in_=b1.rearrange("e (r p) -> (e r) p", p=P))
+        temp = const.tile([P, 1], BF16)
+        nc.scalar.dma_start(out=temp[:], in_=temperature.partition_broadcast(P))
+
+        raws = {}
+        for u in range(LOAD_AHEAD):
+            raws[u] = load_chunk(u)
+
+        identity = const.tile([P, P], BF16)
+        make_identity(nc, identity[:])
+
+        x_t = psum_setup.tile([P, E, PACK, TOKENS], BF16)
+        for e in range(E):
+            for t in range(PACK):
+                nc.tensor.transpose(x_t[:, e, t, :], x_rows[:, e, t * P : (t + 1) * P], identity[:])
+        x_grouped = const.tile([P, E, TOKENS, PACK], BF16, align_bytes=64)
+        nc.vector.tensor_copy(out=x_grouped[:], in_=x_t[:].rearrange("p e t n -> p e n t"))
+        x_words = const.tile([P, E * TOKENS], U32, align_bytes=64)
+        x_scales = const.tile([P, E * TOKENS], U8, align_bytes=64)
+        nc.vector.quantize_mx(
+            out=x_words[:].bitcast(FP8X4),
+            scales=x_scales[:],
+            in_=x_grouped[:].rearrange("p e n t -> p (e n t)"),
+        )
+
+        b1_t_psum = psum_setup.tile([P, P], BF16)
+        nc.tensor.transpose(b1_t_psum[:], b1_rows[:], identity[:])
+        b1_t = const.tile([P, P], F32)
+        nc.vector.tensor_copy(out=b1_t[:], in_=b1_t_psum[:])
+
+        temp_clamped = const.tile([P, 1], F32)
+        nc.vector.tensor_scalar_min(out=temp_clamped[:], in0=temp[:], scalar1=CLAMP_MAX)
+        logit_scale = const.tile([P, 1], F32)
+        nc.scalar.activation(out=logit_scale[:], in_=temp_clamped[:], func=ACT.Exp)
+
+        b2_all = const.tile([P, E * D], BF16)
+        b2_scaled = const.tile([P, E * D], F32)
+
+        def first_matmul(e, w1_words, w1_scales):
+            banks = []
+            for q in range(PASSES):
+                h_t = psum_hidden.tile([P, PACK, TOKENS], F32, name="h_t")
+                for t in range(PACK):
+                    columns = slice((q * PACK + t) * P, (q * PACK + t + 1) * P)
+                    nc.tensor.matmul_mx(
+                        out=h_t[:, t, :],
+                        lhsT=w1_words[:, columns].bitcast(FP8X4),
+                        lhsT_scale=w1_scales[:, columns],
+                        rhs=x_words[:, e * TOKENS : (e + 1) * TOKENS].bitcast(FP8X4),
+                        rhs_scale=x_scales[:, e * TOKENS : (e + 1) * TOKENS],
+                        start=True,
+                        stop=True,
+                    )
+                banks.append(h_t)
+            return banks
+
+        def bias_and_relu(e, c, banks):
+            biased = hidden_pool.tile([P, PASSES, TOKENS, PACK], BF16, name="biased")
+            for q in range(PASSES):
+                first = e * (H // P) + (c * PASSES + q) * PACK
+                nc.vector.tensor_tensor(
+                    out=biased[:, q, :, :],
+                    in0=banks[q][:].rearrange("p t n -> p n t"),
+                    in1=b1_t[:, first : first + PACK].unsqueeze(1).to_broadcast([P, TOKENS, PACK]),
+                    op=ALU.add,
+                )
+            h = hidden_pool.tile([P, PASSES * TOKENS * PACK], BF16, name="h", align_bytes=64)
+            nc.vector.tensor_scalar_max(
+                out=h[:], in0=biased[:].rearrange("p q n t -> p (q n t)"), scalar1=0.0
+            )
+            return h
+
+        def quantise_hidden(h):
+            h_words = hidden_pool.tile([P, PASSES * TOKENS], U32, name="h_words", align_bytes=64)
+            h_scales = hidden_pool.tile([P, PASSES * TOKENS], U8, name="h_scales", align_bytes=64)
+            nc.vector.quantize_mx(out=h_words[:].bitcast(FP8X4), scales=h_scales[:], in_=h[:])
+            return h_words, h_scales
+
+        def second_matmul(c, y, h_words, h_scales, w2_words, w2_scales):
+            for q in range(PASSES):
+                g = c * PASSES + q
+                nc.tensor.matmul_mx(
+                    out=y[:],
+                    lhsT=h_words[:, q * TOKENS : (q + 1) * TOKENS].bitcast(FP8X4),
+                    lhsT_scale=h_scales[:, q * TOKENS : (q + 1) * TOKENS],
+                    rhs=w2_words[:, q * D : (q + 1) * D].bitcast(FP8X4),
+                    rhs_scale=w2_scales[:, q * D : (q + 1) * D],
+                    start=(g == 0),
+                    stop=(g == H // K_PASS - 1),
+                )
+
+        def finish(e, y):
+            result = hidden_pool.tile([P, D], F32, name="result")
+            nc.vector.scalar_tensor_tensor(
+                out=result[:],
+                in0=y[:],
+                scalar=logit_scale[:, 0:1],
+                in1=b2_scaled[:, e * D : (e + 1) * D],
+                op0=ALU.mult,
+                op1=ALU.add,
+            )
+            nc.sync.dma_start(out=out[e * TOKENS : (e + 1) * TOKENS, :], in_=result[:])
+
+        groupeds = {}
+        operands = {}
+        hidden_banks = {}
+        ys = {}
+        for u in range(N_CHUNKS + 1):
+            if u + LOAD_AHEAD < N_CHUNKS:
+                raws[u + LOAD_AHEAD] = load_chunk(u + LOAD_AHEAD)
+            if u == B2_LOAD_STEP:
+                nc.sync.dma_start(
+                    out=b2_all[:], in_=b2.rearrange("e d -> (e d)").partition_broadcast(P)
+                )
+            if u == B2_SCALE_STEP:
+                nc.vector.tensor_scalar_mul(
+                    out=b2_scaled[:], in0=b2_all[:], scalar1=logit_scale[:, 0:1]
+                )
+            if u < N_CHUNKS:
+                groupeds[u] = regroup(raws[u])
+            if u == 0:
+                continue
+            e, c, is_w2 = place(u - 1)
+            if is_w2:
+                h = bias_and_relu(e, c, hidden_banks[u - 2])
+            operands[u - 1] = quantise(groupeds[u - 1])
+            if not is_w2:
+                hidden_banks[u - 1] = first_matmul(e, *operands[u - 1])
+            else:
+                if c == 0:
+                    ys[e] = psum_y.tile([P, D], F32, name="y")
+                second_matmul(c, ys[e], *quantise_hidden(h), *operands[u - 1])
+                if c == PAIRS - 1:
+                    finish(e, ys[e])

@@ -21,16 +21,20 @@ TOKENS = 128
 D = 512
 H = 8192
 
-CHUNK = 2048
-PASSES = CHUNK // D
-PAIRS = H // CHUNK
-N_CHUNKS = E * PAIRS * 2
+PIECE = 512
+CHUNK_PIECES = 4
+CHUNK = CHUNK_PIECES * PIECE
+N_CHUNKS = 2 * E * H // CHUNK
+N_PIECES = N_CHUNKS * CHUNK_PIECES
+EXPERT_PIECES = N_PIECES // E
 LOAD_AHEAD = 3
-B2_LOAD_STEP = LOAD_AHEAD
-B2_SCALE_STEP = 2 * LOAD_AHEAD
+W1_DMAS = 2
+FIRST_W1_DMAS = 4
 
-HALF = CHUNK // 2
-VECTOR_WORDS = 384
+VECTOR_WORDS = 176
+
+B2_LOAD_STEP = EXPERT_PIECES // 2
+B2_SCALE_STEP = B2_LOAD_STEP + 2 * CHUNK_PIECES
 
 CLAMP_MAX = math.log(100.0)
 
@@ -41,154 +45,159 @@ def tile_moelayer_k_kernel(tc, x, W1, b1, W2, b2, temperature, out):
     nc = tc.nc
     with ExitStack() as stack:
         stack.enter_context(nc.allow_non_contiguous_dma(reason="temperature: one element a partition"))
+        stack.enter_context(tc.manual_schedule())
         const = stack.enter_context(tc.tile_pool(name="const", bufs=1))
         raw_pool = stack.enter_context(tc.tile_pool(name="raw", bufs=LOAD_AHEAD + 1))
-        grouped_pool = stack.enter_context(tc.tile_pool(name="grouped", bufs=3))
-        operand_pool = stack.enter_context(tc.tile_pool(name="operand", bufs=3))
+        grouped_pool = stack.enter_context(tc.tile_pool(name="grouped", bufs=2 * CHUNK_PIECES))
+        operand_pool = stack.enter_context(tc.tile_pool(name="operand", bufs=CHUNK_PIECES))
         hidden_pool = stack.enter_context(tc.tile_pool(name="hidden", bufs=2))
         psum_setup = stack.enter_context(tc.psum_pool(name="psum_setup", bufs=1))
-        psum_hidden = stack.enter_context(tc.psum_pool(name="psum_hidden", bufs=PASSES))
+        psum_hidden = stack.enter_context(tc.psum_pool(name="psum_hidden", bufs=CHUNK_PIECES))
         psum_y = stack.enter_context(tc.psum_pool(name="psum_y", bufs=E))
 
-        def place(u):
-            return u // (2 * PAIRS), (u // 2) % PAIRS, u % 2 == 1
+        def place(v):
+            chunk = v // CHUNK_PIECES
+            g = (chunk // 2) * CHUNK_PIECES + v % CHUNK_PIECES
+            return g // (H // K_PASS), g % (H // K_PASS), chunk % 2 == 1
 
-        def load_chunk(u):
-            e, c, is_w2 = place(u)
+        def load_chunk(chunk):
+            e, g, is_w2 = place(chunk * CHUNK_PIECES)
             raw = raw_pool.tile([P, PACK, CHUNK], BF16, name="raw")
-            if not is_w2:
-                columns = W1[e, :, c * CHUNK : (c + 1) * CHUNK]
-                nc.sync.dma_start(out=raw[:], in_=columns.rearrange("(t p) w -> p t w", p=P))
-            else:
-                for q in range(PASSES):
-                    first_row = c * CHUNK + q * K_PASS
-                    rows = W2[e, first_row : first_row + K_PASS, :]
+            if is_w2:
+                for q in range(CHUNK_PIECES):
+                    rows = W2[e, (g + q) * K_PASS : (g + q + 1) * K_PASS, :]
                     nc.sync.dma_start(
-                        out=raw[:, :, q * D : (q + 1) * D],
+                        out=raw[:, :, q * PIECE : (q + 1) * PIECE],
                         in_=rows.rearrange("(t p) d -> p t d", p=P),
+                    )
+            else:
+                width = CHUNK // (FIRST_W1_DMAS if chunk == 0 else W1_DMAS)
+                for first in range(0, CHUNK, width):
+                    columns = W1[e, :, g * PIECE + first : g * PIECE + first + width]
+                    nc.sync.dma_start(
+                        out=raw[:, :, first : first + width],
+                        in_=columns.rearrange("(t p) w -> p t w", p=P),
                     )
             return raw
 
-        def regroup(raw):
-            grouped = grouped_pool.tile([P, CHUNK, PACK], BF16, name="grouped", align_bytes=64)
+        def regroup(raw, q):
+            grouped = grouped_pool.tile([P, PIECE, PACK], BF16, name="grouped", align_bytes=64)
 
             def views(first, last):
                 return (
                     grouped[:, first:last, :].rearrange("p (c i) t -> p c t i", i=4),
-                    raw[:, :, first:last].rearrange("p t (c i) -> p c t i", i=4),
+                    raw[:, :, q * PIECE + first : q * PIECE + last].rearrange(
+                        "p t (c i) -> p c t i", i=4
+                    ),
                 )
 
-            for half in range(0, CHUNK, HALF):
-                to, frm = views(half, half + VECTOR_WORDS)
-                nc.vector.tensor_copy(out=to, in_=frm)
-                to, frm = views(half + VECTOR_WORDS, half + HALF)
-                nc.scalar.copy(out=to, in_=frm)
+            to, frm = views(0, VECTOR_WORDS)
+            nc.vector.tensor_copy(out=to, in_=frm)
+            to, frm = views(VECTOR_WORDS, PIECE)
+            nc.scalar.copy(out=to, in_=frm)
             return grouped
 
         def quantise(grouped):
-            words = operand_pool.tile([P, CHUNK], U32, name="words", align_bytes=64)
-            scales = operand_pool.tile([P, CHUNK], U8, name="scales", align_bytes=64)
-            for half in range(0, CHUNK, HALF):
-                nc.vector.quantize_mx(
-                    out=words[:, half : half + HALF].bitcast(FP8X4),
-                    scales=scales[:, half : half + HALF],
-                    in_=grouped[:, half : half + HALF, :].rearrange("p w t -> p (w t)"),
-                )
+            words = operand_pool.tile([P, PIECE], U32, name="words", align_bytes=64)
+            scales = operand_pool.tile([P, PIECE], U8, name="scales", align_bytes=64)
+            nc.vector.quantize_mx(
+                out=words[:].bitcast(FP8X4),
+                scales=scales[:],
+                in_=grouped[:].rearrange("p w t -> p (w t)"),
+            )
             return words, scales
 
+        temp = const.tile([P, 1], BF16)
+        nc.scalar.dma_start(out=temp[:], in_=temperature.partition_broadcast(P))
         x_rows = const.tile([P, E, D], BF16)
         nc.scalar.dma_start(out=x_rows[:], in_=x.rearrange("(e n) k -> n e k", e=E))
         b1_rows = const.tile([P, P], BF16)
         nc.scalar.dma_start(out=b1_rows[:], in_=b1.rearrange("e (r p) -> (e r) p", p=P))
-        temp = const.tile([P, 1], BF16)
-        nc.scalar.dma_start(out=temp[:], in_=temperature.partition_broadcast(P))
 
         raws = {}
-        for u in range(LOAD_AHEAD):
-            raws[u] = load_chunk(u)
+        for chunk in range(LOAD_AHEAD):
+            raws[chunk] = load_chunk(chunk)
 
         identity = const.tile([P, P], BF16)
         make_identity(nc, identity[:])
-
-        x_t = psum_setup.tile([P, E, PACK, TOKENS], BF16)
-        for e in range(E):
-            for t in range(PACK):
-                nc.tensor.transpose(x_t[:, e, t, :], x_rows[:, e, t * P : (t + 1) * P], identity[:])
-        x_grouped = const.tile([P, E, TOKENS, PACK], BF16, align_bytes=64)
-        nc.vector.tensor_copy(out=x_grouped[:], in_=x_t[:].rearrange("p e t n -> p e n t"))
-        x_words = const.tile([P, E * TOKENS], U32, align_bytes=64)
-        x_scales = const.tile([P, E * TOKENS], U8, align_bytes=64)
-        nc.vector.quantize_mx(
-            out=x_words[:].bitcast(FP8X4),
-            scales=x_scales[:],
-            in_=x_grouped[:].rearrange("p e n t -> p (e n t)"),
-        )
-
-        b1_t_psum = psum_setup.tile([P, P], BF16)
-        nc.tensor.transpose(b1_t_psum[:], b1_rows[:], identity[:])
-        b1_t = const.tile([P, P], F32)
-        nc.vector.tensor_copy(out=b1_t[:], in_=b1_t_psum[:])
 
         temp_clamped = const.tile([P, 1], F32)
         nc.vector.tensor_scalar_min(out=temp_clamped[:], in0=temp[:], scalar1=CLAMP_MAX)
         logit_scale = const.tile([P, 1], F32)
         nc.scalar.activation(out=logit_scale[:], in_=temp_clamped[:], func=ACT.Exp)
 
+        x_words = const.tile([P, E * TOKENS], U32, align_bytes=64)
+        x_scales = const.tile([P, E * TOKENS], U8, align_bytes=64)
+        b1_t = const.tile([P, P], F32)
+
+        def prepare_x_and_b1():
+            x_t = psum_setup.tile([P, E, PACK, TOKENS], BF16)
+            for e in range(E):
+                for t in range(PACK):
+                    nc.tensor.transpose(
+                        x_t[:, e, t, :], x_rows[:, e, t * P : (t + 1) * P], identity[:]
+                    )
+            x_grouped = const.tile([P, E, TOKENS, PACK], BF16, align_bytes=64)
+            nc.vector.tensor_copy(out=x_grouped[:], in_=x_t[:].rearrange("p e t n -> p e n t"))
+            b1_t_psum = psum_setup.tile([P, P], BF16)
+            nc.tensor.transpose(b1_t_psum[:], b1_rows[:], identity[:])
+            nc.vector.tensor_copy(out=b1_t[:], in_=b1_t_psum[:])
+            nc.vector.quantize_mx(
+                out=x_words[:].bitcast(FP8X4),
+                scales=x_scales[:],
+                in_=x_grouped[:].rearrange("p e n t -> p (e n t)"),
+            )
+
         b2_all = const.tile([P, E * D], BF16)
         b2_scaled = const.tile([P, E * D], F32)
 
         def first_matmul(e, w1_words, w1_scales):
-            banks = []
-            for q in range(PASSES):
-                h_t = psum_hidden.tile([P, PACK, TOKENS], F32, name="h_t")
-                for t in range(PACK):
-                    columns = slice((q * PACK + t) * P, (q * PACK + t + 1) * P)
-                    nc.tensor.matmul_mx(
-                        out=h_t[:, t, :],
-                        lhsT=w1_words[:, columns].bitcast(FP8X4),
-                        lhsT_scale=w1_scales[:, columns],
-                        rhs=x_words[:, e * TOKENS : (e + 1) * TOKENS].bitcast(FP8X4),
-                        rhs_scale=x_scales[:, e * TOKENS : (e + 1) * TOKENS],
-                        start=True,
-                        stop=True,
-                    )
-                banks.append(h_t)
-            return banks
-
-        def bias_and_relu(e, c, banks):
-            biased = hidden_pool.tile([P, PASSES, TOKENS, PACK], BF16, name="biased")
-            for q in range(PASSES):
-                first = e * (H // P) + (c * PASSES + q) * PACK
-                nc.vector.tensor_tensor(
-                    out=biased[:, q, :, :],
-                    in0=banks[q][:].rearrange("p t n -> p n t"),
-                    in1=b1_t[:, first : first + PACK].unsqueeze(1).to_broadcast([P, TOKENS, PACK]),
-                    op=ALU.add,
+            h_t = psum_hidden.tile([P, PACK, TOKENS], F32, name="h_t")
+            for t in range(PACK):
+                nc.tensor.matmul_mx(
+                    out=h_t[:, t, :],
+                    lhsT=w1_words[:, t * P : (t + 1) * P].bitcast(FP8X4),
+                    lhsT_scale=w1_scales[:, t * P : (t + 1) * P],
+                    rhs=x_words[:, e * TOKENS : (e + 1) * TOKENS].bitcast(FP8X4),
+                    rhs_scale=x_scales[:, e * TOKENS : (e + 1) * TOKENS],
+                    start=True,
+                    stop=True,
                 )
-            h = hidden_pool.tile([P, PASSES * TOKENS * PACK], BF16, name="h", align_bytes=64)
+            return h_t
+
+        def add_bias(e, g, h_t, biased):
+            first = e * (H // P) + g * PACK
+            nc.vector.tensor_tensor(
+                out=biased[:, g % CHUNK_PIECES, :, :],
+                in0=h_t[:].rearrange("p t n -> p n t"),
+                in1=b1_t[:, first : first + PACK].unsqueeze(1).to_broadcast([P, TOKENS, PACK]),
+                op=ALU.add,
+            )
+
+        def relu(biased):
+            h = hidden_pool.tile([P, CHUNK_PIECES * TOKENS * PACK], BF16, name="h", align_bytes=64)
             nc.vector.tensor_scalar_max(
                 out=h[:], in0=biased[:].rearrange("p q n t -> p (q n t)"), scalar1=0.0
             )
             return h
 
         def quantise_hidden(h):
-            h_words = hidden_pool.tile([P, PASSES * TOKENS], U32, name="h_words", align_bytes=64)
-            h_scales = hidden_pool.tile([P, PASSES * TOKENS], U8, name="h_scales", align_bytes=64)
+            h_words = hidden_pool.tile([P, CHUNK_PIECES * TOKENS], U32, name="h_words", align_bytes=64)
+            h_scales = hidden_pool.tile([P, CHUNK_PIECES * TOKENS], U8, name="h_scales", align_bytes=64)
             nc.vector.quantize_mx(out=h_words[:].bitcast(FP8X4), scales=h_scales[:], in_=h[:])
             return h_words, h_scales
 
-        def second_matmul(c, y, h_words, h_scales, w2_words, w2_scales):
-            for q in range(PASSES):
-                g = c * PASSES + q
-                nc.tensor.matmul_mx(
-                    out=y[:],
-                    lhsT=h_words[:, q * TOKENS : (q + 1) * TOKENS].bitcast(FP8X4),
-                    lhsT_scale=h_scales[:, q * TOKENS : (q + 1) * TOKENS],
-                    rhs=w2_words[:, q * D : (q + 1) * D].bitcast(FP8X4),
-                    rhs_scale=w2_scales[:, q * D : (q + 1) * D],
-                    start=(g == 0),
-                    stop=(g == H // K_PASS - 1),
-                )
+        def second_matmul(g, y, h_words, h_scales, w2_words, w2_scales):
+            tokens = slice((g % CHUNK_PIECES) * TOKENS, (g % CHUNK_PIECES + 1) * TOKENS)
+            nc.tensor.matmul_mx(
+                out=y[:],
+                lhsT=h_words[:, tokens].bitcast(FP8X4),
+                lhsT_scale=h_scales[:, tokens],
+                rhs=w2_words[:].bitcast(FP8X4),
+                rhs_scale=w2_scales[:],
+                start=(g == 0),
+                stop=(g == H // K_PASS - 1),
+            )
 
         def finish(e, y):
             result = hidden_pool.tile([P, D], F32, name="result")
@@ -204,32 +213,48 @@ def tile_moelayer_k_kernel(tc, x, W1, b1, W2, b2, temperature, out):
 
         groupeds = {}
         operands = {}
-        hidden_banks = {}
-        ys = {}
-        for u in range(N_CHUNKS + 1):
-            if u + LOAD_AHEAD < N_CHUNKS:
-                raws[u + LOAD_AHEAD] = load_chunk(u + LOAD_AHEAD)
-            if u == B2_LOAD_STEP:
+        products = {}
+        for v in range(N_PIECES + 3):
+            if v < N_PIECES:
+                chunk = v // CHUNK_PIECES
+                if v % CHUNK_PIECES == 0 and chunk + LOAD_AHEAD < N_CHUNKS:
+                    raws[chunk + LOAD_AHEAD] = load_chunk(chunk + LOAD_AHEAD)
+                groupeds[v] = regroup(raws[chunk], v % CHUNK_PIECES)
+            if v == 0:
+                prepare_x_and_b1()
+            if v == B2_LOAD_STEP:
                 nc.sync.dma_start(
                     out=b2_all[:], in_=b2.rearrange("e d -> (e d)").partition_broadcast(P)
                 )
-            if u == B2_SCALE_STEP:
+            if v == B2_SCALE_STEP:
                 nc.vector.tensor_scalar_mul(
                     out=b2_scaled[:], in0=b2_all[:], scalar1=logit_scale[:, 0:1]
                 )
-            if u < N_CHUNKS:
-                groupeds[u] = regroup(raws[u])
-            if u == 0:
-                continue
-            e, c, is_w2 = place(u - 1)
-            if is_w2:
-                h = bias_and_relu(e, c, hidden_banks[u - 2])
-            operands[u - 1] = quantise(groupeds[u - 1])
-            if not is_w2:
-                hidden_banks[u - 1] = first_matmul(e, *operands[u - 1])
-            else:
-                if c == 0:
-                    ys[e] = psum_y.tile([P, D], F32, name="y")
-                second_matmul(c, ys[e], *quantise_hidden(h), *operands[u - 1])
-                if c == PAIRS - 1:
-                    finish(e, ys[e])
+
+            if v >= 3:
+                e, g, is_w2 = place(v - 3)
+                if not is_w2 and g % CHUNK_PIECES == CHUNK_PIECES - 1:
+                    h_operand = quantise_hidden(h)
+                if is_w2 and g == H // K_PASS - 1:
+                    finish(e, y)
+
+            if 1 <= v <= N_PIECES:
+                e, g, is_w2 = place(v - 1)
+                operands[v - 1] = quantise(groupeds[v - 1])
+                if not is_w2:
+                    products[v - 1] = first_matmul(e, *operands[v - 1])
+
+            if 2 <= v <= N_PIECES + 1:
+                e, g, is_w2 = place(v - 2)
+                if not is_w2:
+                    if g % CHUNK_PIECES == 0:
+                        biased = hidden_pool.tile(
+                            [P, CHUNK_PIECES, TOKENS, PACK], BF16, name="biased"
+                        )
+                    add_bias(e, g, products[v - 2], biased)
+                    if g % CHUNK_PIECES == CHUNK_PIECES - 1:
+                        h = relu(biased)
+                else:
+                    if g == 0:
+                        y = psum_y.tile([P, D], F32, name="y")
+                    second_matmul(g, y, *h_operand, *operands[v - 2])

@@ -20,21 +20,19 @@ E = 2
 TOKENS = 128
 D = 512
 H = 8192
+PASSES = H // K_PASS
 
-PIECE = 512
-CHUNK_PIECES = 4
-CHUNK = CHUNK_PIECES * PIECE
-N_CHUNKS = 2 * E * H // CHUNK
-N_PIECES = N_CHUNKS * CHUNK_PIECES
-EXPERT_PIECES = N_PIECES // E
-LOAD_AHEAD = 3
-W1_DMAS = 2
-FIRST_W1_DMAS = 4
+UNIT = 1024
+UNIT_PASSES = UNIT // D
+EXPERT_UNITS = H // UNIT
+N_UNITS = E * EXPERT_UNITS
+LEAD = 3
+LOAD_AHEAD = 7
 
-VECTOR_WORDS = 176
+VECTOR_WORDS = 336
 
-B2_LOAD_STEP = EXPERT_PIECES // 2
-B2_SCALE_STEP = B2_LOAD_STEP + 2 * CHUNK_PIECES
+B2_LOAD_STEP = N_UNITS // 2
+B2_SCALE_STEP = B2_LOAD_STEP + 4
 
 CLAMP_MAX = math.log(100.0)
 
@@ -48,64 +46,61 @@ def tile_moelayer_k_kernel(tc, x, W1, b1, W2, b2, temperature, out):
         stack.enter_context(tc.manual_schedule())
         const = stack.enter_context(tc.tile_pool(name="const", bufs=1))
         raw_pool = stack.enter_context(tc.tile_pool(name="raw", bufs=LOAD_AHEAD + 1))
-        grouped_pool = stack.enter_context(tc.tile_pool(name="grouped", bufs=2 * CHUNK_PIECES))
-        operand_pool = stack.enter_context(tc.tile_pool(name="operand", bufs=CHUNK_PIECES))
-        hidden_pool = stack.enter_context(tc.tile_pool(name="hidden", bufs=2))
+        grouped_pool = stack.enter_context(tc.tile_pool(name="grouped", bufs=4))
+        operand_pool = stack.enter_context(tc.tile_pool(name="operand", bufs=3))
+        hidden_pool = stack.enter_context(tc.tile_pool(name="hidden", bufs=LEAD + 1))
         psum_setup = stack.enter_context(tc.psum_pool(name="psum_setup", bufs=1))
-        psum_hidden = stack.enter_context(tc.psum_pool(name="psum_hidden", bufs=CHUNK_PIECES))
+        psum_hidden = stack.enter_context(tc.psum_pool(name="psum_hidden", bufs=2 * UNIT_PASSES))
         psum_y = stack.enter_context(tc.psum_pool(name="psum_y", bufs=E))
 
-        def place(v):
-            chunk = v // CHUNK_PIECES
-            g = (chunk // 2) * CHUNK_PIECES + v % CHUNK_PIECES
-            return g // (H // K_PASS), g % (H // K_PASS), chunk % 2 == 1
-
-        def load_chunk(chunk):
-            e, g, is_w2 = place(chunk * CHUNK_PIECES)
-            raw = raw_pool.tile([P, PACK, CHUNK], BF16, name="raw")
-            if is_w2:
-                for q in range(CHUNK_PIECES):
-                    rows = W2[e, (g + q) * K_PASS : (g + q + 1) * K_PASS, :]
-                    nc.sync.dma_start(
-                        out=raw[:, :, q * PIECE : (q + 1) * PIECE],
-                        in_=rows.rearrange("(t p) d -> p t d", p=P),
-                    )
+        def load_unit(weight, j):
+            e, i = j // EXPERT_UNITS, j % EXPERT_UNITS
+            raw = raw_pool.tile([P, PACK, UNIT], BF16, name="raw")
+            if weight == "W1":
+                columns = W1[e, :, i * UNIT : (i + 1) * UNIT]
+                nc.sync.dma_start(out=raw[:], in_=columns.rearrange("(t p) w -> p t w", p=P))
             else:
-                width = CHUNK // (FIRST_W1_DMAS if chunk == 0 else W1_DMAS)
-                for first in range(0, CHUNK, width):
-                    columns = W1[e, :, g * PIECE + first : g * PIECE + first + width]
+                for q in range(UNIT_PASSES):
+                    g = i * UNIT_PASSES + q
+                    rows = W2[e, g * K_PASS : (g + 1) * K_PASS, :]
                     nc.sync.dma_start(
-                        out=raw[:, :, first : first + width],
-                        in_=columns.rearrange("(t p) w -> p t w", p=P),
+                        out=raw[:, :, q * D : (q + 1) * D],
+                        in_=rows.rearrange("(t p) d -> p t d", p=P),
                     )
             return raw
 
-        def regroup(raw, q):
-            grouped = grouped_pool.tile([P, PIECE, PACK], BF16, name="grouped", align_bytes=64)
+        def regroup(raw):
+            grouped = grouped_pool.tile([P, UNIT, PACK], BF16, name="grouped", align_bytes=64)
 
             def views(first, last):
                 return (
                     grouped[:, first:last, :].rearrange("p (c i) t -> p c t i", i=4),
-                    raw[:, :, q * PIECE + first : q * PIECE + last].rearrange(
-                        "p t (c i) -> p c t i", i=4
-                    ),
+                    raw[:, :, first:last].rearrange("p t (c i) -> p c t i", i=4),
                 )
 
             to, frm = views(0, VECTOR_WORDS)
             nc.vector.tensor_copy(out=to, in_=frm)
-            to, frm = views(VECTOR_WORDS, PIECE)
+            to, frm = views(VECTOR_WORDS, UNIT)
             nc.scalar.copy(out=to, in_=frm)
             return grouped
 
         def quantise(grouped):
-            words = operand_pool.tile([P, PIECE], U32, name="words", align_bytes=64)
-            scales = operand_pool.tile([P, PIECE], U8, name="scales", align_bytes=64)
+            words = operand_pool.tile([P, UNIT], U32, name="words", align_bytes=64)
+            scales = operand_pool.tile([P, UNIT], U8, name="scales", align_bytes=64)
             nc.vector.quantize_mx(
                 out=words[:].bitcast(FP8X4),
                 scales=scales[:],
                 in_=grouped[:].rearrange("p w t -> p (w t)"),
             )
             return words, scales
+
+        stream = [("W1", j) for j in range(LEAD)]
+        for j in range(N_UNITS - LEAD):
+            stream.extend([("W2", j), ("W1", j + LEAD)])
+        stream.extend([("W2", j) for j in range(N_UNITS - LEAD, N_UNITS)])
+
+        def unit_at(s):
+            return stream[s] if 0 <= s < len(stream) else (None, None)
 
         temp = const.tile([P, 1], BF16)
         nc.scalar.dma_start(out=temp[:], in_=temperature.partition_broadcast(P))
@@ -115,8 +110,8 @@ def tile_moelayer_k_kernel(tc, x, W1, b1, W2, b2, temperature, out):
         nc.scalar.dma_start(out=b1_rows[:], in_=b1.rearrange("e (r p) -> (e r) p", p=P))
 
         raws = {}
-        for chunk in range(LOAD_AHEAD):
-            raws[chunk] = load_chunk(chunk)
+        for s in range(LOAD_AHEAD):
+            raws[s] = load_unit(*stream[s])
 
         identity = const.tile([P, P], BF16)
         make_identity(nc, identity[:])
@@ -151,53 +146,62 @@ def tile_moelayer_k_kernel(tc, x, W1, b1, W2, b2, temperature, out):
         b2_all = const.tile([P, E * D], BF16)
         b2_scaled = const.tile([P, E * D], F32)
 
-        def first_matmul(e, w1_words, w1_scales):
-            h_t = psum_hidden.tile([P, PACK, TOKENS], F32, name="h_t")
-            for t in range(PACK):
-                nc.tensor.matmul_mx(
-                    out=h_t[:, t, :],
-                    lhsT=w1_words[:, t * P : (t + 1) * P].bitcast(FP8X4),
-                    lhsT_scale=w1_scales[:, t * P : (t + 1) * P],
-                    rhs=x_words[:, e * TOKENS : (e + 1) * TOKENS].bitcast(FP8X4),
-                    rhs_scale=x_scales[:, e * TOKENS : (e + 1) * TOKENS],
-                    start=True,
-                    stop=True,
-                )
-            return h_t
+        def first_matmul(j, w1_words, w1_scales):
+            tokens = slice((j // EXPERT_UNITS) * TOKENS, (j // EXPERT_UNITS + 1) * TOKENS)
+            product = []
+            for q in range(UNIT_PASSES):
+                bank = psum_hidden.tile([P, PACK, TOKENS], F32, name="bank")
+                for t in range(PACK):
+                    columns = slice((q * PACK + t) * P, (q * PACK + t + 1) * P)
+                    nc.tensor.matmul_mx(
+                        out=bank[:, t, :],
+                        lhsT=w1_words[:, columns].bitcast(FP8X4),
+                        lhsT_scale=w1_scales[:, columns],
+                        rhs=x_words[:, tokens].bitcast(FP8X4),
+                        rhs_scale=x_scales[:, tokens],
+                        start=True,
+                        stop=True,
+                    )
+                product.append(bank)
+            return product
 
-        def add_bias(e, g, h_t, biased):
-            first = e * (H // P) + g * PACK
-            nc.vector.tensor_tensor(
-                out=biased[:, g % CHUNK_PIECES, :, :],
-                in0=h_t[:].rearrange("p t n -> p n t"),
-                in1=b1_t[:, first : first + PACK].unsqueeze(1).to_broadcast([P, TOKENS, PACK]),
-                op=ALU.add,
-            )
+        def add_bias(j, product):
+            biased = hidden_pool.tile([P, UNIT_PASSES, TOKENS, PACK], BF16, name="biased")
+            for q in range(UNIT_PASSES):
+                first = (j * UNIT_PASSES + q) * PACK
+                nc.vector.tensor_tensor(
+                    out=biased[:, q, :, :],
+                    in0=product[q][:].rearrange("p t n -> p n t"),
+                    in1=b1_t[:, first : first + PACK].unsqueeze(1).to_broadcast([P, TOKENS, PACK]),
+                    op=ALU.add,
+                )
+            return biased
 
         def relu(biased):
-            h = hidden_pool.tile([P, CHUNK_PIECES * TOKENS * PACK], BF16, name="h", align_bytes=64)
+            h = hidden_pool.tile([P, UNIT_PASSES * TOKENS * PACK], BF16, name="h", align_bytes=64)
             nc.vector.tensor_scalar_max(
                 out=h[:], in0=biased[:].rearrange("p q n t -> p (q n t)"), scalar1=0.0
             )
             return h
 
         def quantise_hidden(h):
-            h_words = hidden_pool.tile([P, CHUNK_PIECES * TOKENS], U32, name="h_words", align_bytes=64)
-            h_scales = hidden_pool.tile([P, CHUNK_PIECES * TOKENS], U8, name="h_scales", align_bytes=64)
+            h_words = hidden_pool.tile([P, UNIT_PASSES * TOKENS], U32, name="h_words", align_bytes=64)
+            h_scales = hidden_pool.tile([P, UNIT_PASSES * TOKENS], U8, name="h_scales", align_bytes=64)
             nc.vector.quantize_mx(out=h_words[:].bitcast(FP8X4), scales=h_scales[:], in_=h[:])
             return h_words, h_scales
 
-        def second_matmul(g, y, h_words, h_scales, w2_words, w2_scales):
-            tokens = slice((g % CHUNK_PIECES) * TOKENS, (g % CHUNK_PIECES + 1) * TOKENS)
-            nc.tensor.matmul_mx(
-                out=y[:],
-                lhsT=h_words[:, tokens].bitcast(FP8X4),
-                lhsT_scale=h_scales[:, tokens],
-                rhs=w2_words[:].bitcast(FP8X4),
-                rhs_scale=w2_scales[:],
-                start=(g == 0),
-                stop=(g == H // K_PASS - 1),
-            )
+        def second_matmul(j, y, h_words, h_scales, w2_words, w2_scales):
+            for q in range(UNIT_PASSES):
+                g = (j % EXPERT_UNITS) * UNIT_PASSES + q
+                nc.tensor.matmul_mx(
+                    out=y[:],
+                    lhsT=h_words[:, q * TOKENS : (q + 1) * TOKENS].bitcast(FP8X4),
+                    lhsT_scale=h_scales[:, q * TOKENS : (q + 1) * TOKENS],
+                    rhs=w2_words[:, q * D : (q + 1) * D].bitcast(FP8X4),
+                    rhs_scale=w2_scales[:, q * D : (q + 1) * D],
+                    start=(g == 0),
+                    stop=(g == PASSES - 1),
+                )
 
         def finish(e, y):
             result = hidden_pool.tile([P, D], F32, name="result")
@@ -212,49 +216,47 @@ def tile_moelayer_k_kernel(tc, x, W1, b1, W2, b2, temperature, out):
             nc.sync.dma_start(out=out[e * TOKENS : (e + 1) * TOKENS, :], in_=result[:])
 
         groupeds = {}
-        operands = {}
         products = {}
-        for v in range(N_PIECES + 3):
-            if v < N_PIECES:
-                chunk = v // CHUNK_PIECES
-                if v % CHUNK_PIECES == 0 and chunk + LOAD_AHEAD < N_CHUNKS:
-                    raws[chunk + LOAD_AHEAD] = load_chunk(chunk + LOAD_AHEAD)
-                groupeds[v] = regroup(raws[chunk], v % CHUNK_PIECES)
-            if v == 0:
+        biaseds = {}
+        hs = {}
+        h_operands = {}
+        ys = {}
+        for s in range(len(stream) + 2):
+            if s + LOAD_AHEAD < len(stream):
+                raws[s + LOAD_AHEAD] = load_unit(*stream[s + LOAD_AHEAD])
+            if s < len(stream):
+                groupeds[s] = regroup(raws[s])
+            if s == 0:
                 prepare_x_and_b1()
-            if v == B2_LOAD_STEP:
+            if s == B2_LOAD_STEP:
                 nc.sync.dma_start(
                     out=b2_all[:], in_=b2.rearrange("e d -> (e d)").partition_broadcast(P)
                 )
-            if v == B2_SCALE_STEP:
+            if s == B2_SCALE_STEP:
                 nc.vector.tensor_scalar_mul(
                     out=b2_scaled[:], in0=b2_all[:], scalar1=logit_scale[:, 0:1]
                 )
 
-            if v >= 3:
-                e, g, is_w2 = place(v - 3)
-                if not is_w2 and g % CHUNK_PIECES == CHUNK_PIECES - 1:
-                    h_operand = quantise_hidden(h)
-                if is_w2 and g == H // K_PASS - 1:
-                    finish(e, y)
+            weight, j = unit_at(s - 4)
+            if weight == "W1":
+                h_operands[j] = quantise_hidden(hs[j])
 
-            if 1 <= v <= N_PIECES:
-                e, g, is_w2 = place(v - 1)
-                operands[v - 1] = quantise(groupeds[v - 1])
-                if not is_w2:
-                    products[v - 1] = first_matmul(e, *operands[v - 1])
+            weight, j = unit_at(s - 3)
+            if weight == "W1":
+                biaseds[j] = add_bias(j, products[j])
 
-            if 2 <= v <= N_PIECES + 1:
-                e, g, is_w2 = place(v - 2)
-                if not is_w2:
-                    if g % CHUNK_PIECES == 0:
-                        biased = hidden_pool.tile(
-                            [P, CHUNK_PIECES, TOKENS, PACK], BF16, name="biased"
-                        )
-                    add_bias(e, g, products[v - 2], biased)
-                    if g % CHUNK_PIECES == CHUNK_PIECES - 1:
-                        h = relu(biased)
-                else:
-                    if g == 0:
-                        y = psum_y.tile([P, D], F32, name="y")
-                    second_matmul(g, y, *h_operand, *operands[v - 2])
+            weight, j = unit_at(s - 1)
+            if weight == "W1":
+                products[j] = first_matmul(j, *quantise(groupeds[s - 1]))
+            if weight == "W2":
+                if j % EXPERT_UNITS == 0:
+                    ys[j // EXPERT_UNITS] = psum_y.tile([P, D], F32, name="y")
+                second_matmul(j, ys[j // EXPERT_UNITS], *h_operands[j], *quantise(groupeds[s - 1]))
+
+            weight, j = unit_at(s - 3)
+            if weight == "W1":
+                hs[j] = relu(biaseds[j])
+
+            weight, j = unit_at(s - 2)
+            if weight == "W2" and j % EXPERT_UNITS == EXPERT_UNITS - 1:
+                finish(j // EXPERT_UNITS, ys[j // EXPERT_UNITS])

import math
from contextlib import ExitStack

import concourse.mybir as mybir
from concourse.masks import make_identity

BF16 = mybir.dt.bfloat16
F32 = mybir.dt.float32
U32 = mybir.dt.uint32
U8 = mybir.dt.uint8
FP8X4 = mybir.dt.float8_e4m3fn_x4
ALU = mybir.AluOpType
ACT = mybir.ActivationFunctionType

P = 128
PACK = 4
K_PASS = P * PACK

E = 2
TOKENS = 128
D = 512
H = 8192
PASSES = H // K_PASS

UNIT = 1024
UNIT_PASSES = UNIT // D
EXPERT_UNITS = H // UNIT
N_UNITS = E * EXPERT_UNITS
LEAD = 3
LOAD_AHEAD = 7

VECTOR_WORDS = 336

B2_LOAD_STEP = N_UNITS // 2
B2_SCALE_STEP = B2_LOAD_STEP + 4

CLAMP_MAX = math.log(100.0)

FLOPS = 2 * (2 * E * TOKENS * D * H)


def tile_moelayer_k_kernel(tc, x, W1, b1, W2, b2, temperature, out):
    nc = tc.nc
    with ExitStack() as stack:
        stack.enter_context(nc.allow_non_contiguous_dma(reason="temperature: one element a partition"))
        stack.enter_context(tc.manual_schedule())
        const = stack.enter_context(tc.tile_pool(name="const", bufs=1))
        raw_pool = stack.enter_context(tc.tile_pool(name="raw", bufs=LOAD_AHEAD + 1))
        grouped_pool = stack.enter_context(tc.tile_pool(name="grouped", bufs=4))
        operand_pool = stack.enter_context(tc.tile_pool(name="operand", bufs=3))
        hidden_pool = stack.enter_context(tc.tile_pool(name="hidden", bufs=LEAD + 1))
        psum_setup = stack.enter_context(tc.psum_pool(name="psum_setup", bufs=1))
        psum_hidden = stack.enter_context(tc.psum_pool(name="psum_hidden", bufs=2 * UNIT_PASSES))
        psum_y = stack.enter_context(tc.psum_pool(name="psum_y", bufs=E))

        def load_unit(weight, j):
            e, i = j // EXPERT_UNITS, j % EXPERT_UNITS
            raw = raw_pool.tile([P, PACK, UNIT], BF16, name="raw")
            if weight == "W1":
                columns = W1[e, :, i * UNIT : (i + 1) * UNIT]
                nc.sync.dma_start(out=raw[:], in_=columns.rearrange("(t p) w -> p t w", p=P))
            else:
                for q in range(UNIT_PASSES):
                    g = i * UNIT_PASSES + q
                    rows = W2[e, g * K_PASS : (g + 1) * K_PASS, :]
                    nc.sync.dma_start(
                        out=raw[:, :, q * D : (q + 1) * D],
                        in_=rows.rearrange("(t p) d -> p t d", p=P),
                    )
            return raw

        def regroup(raw):
            grouped = grouped_pool.tile([P, UNIT, PACK], BF16, name="grouped", align_bytes=64)

            def views(first, last):
                return (
                    grouped[:, first:last, :].rearrange("p (c i) t -> p c t i", i=4),
                    raw[:, :, first:last].rearrange("p t (c i) -> p c t i", i=4),
                )

            to, frm = views(0, VECTOR_WORDS)
            nc.vector.tensor_copy(out=to, in_=frm)
            to, frm = views(VECTOR_WORDS, UNIT)
            nc.scalar.copy(out=to, in_=frm)
            return grouped

        def quantise(grouped):
            words = operand_pool.tile([P, UNIT], U32, name="words", align_bytes=64)
            scales = operand_pool.tile([P, UNIT], U8, name="scales", align_bytes=64)
            nc.vector.quantize_mx(
                out=words[:].bitcast(FP8X4),
                scales=scales[:],
                in_=grouped[:].rearrange("p w t -> p (w t)"),
            )
            return words, scales

        stream = [("W1", j) for j in range(LEAD)]
        for j in range(N_UNITS - LEAD):
            stream.extend([("W2", j), ("W1", j + LEAD)])
        stream.extend([("W2", j) for j in range(N_UNITS - LEAD, N_UNITS)])

        def unit_at(s):
            return stream[s] if 0 <= s < len(stream) else (None, None)

        temp = const.tile([P, 1], BF16)
        nc.scalar.dma_start(out=temp[:], in_=temperature.partition_broadcast(P))
        x_rows = const.tile([P, E, D], BF16)
        nc.scalar.dma_start(out=x_rows[:], in_=x.rearrange("(e n) k -> n e k", e=E))
        b1_rows = const.tile([P, P], BF16)
        nc.scalar.dma_start(out=b1_rows[:], in_=b1.rearrange("e (r p) -> (e r) p", p=P))

        raws = {}
        for s in range(LOAD_AHEAD):
            raws[s] = load_unit(*stream[s])

        identity = const.tile([P, P], BF16)
        make_identity(nc, identity[:])

        temp_clamped = const.tile([P, 1], F32)
        nc.vector.tensor_scalar_min(out=temp_clamped[:], in0=temp[:], scalar1=CLAMP_MAX)
        logit_scale = const.tile([P, 1], F32)
        nc.scalar.activation(out=logit_scale[:], in_=temp_clamped[:], func=ACT.Exp)

        x_words = const.tile([P, E * TOKENS], U32, align_bytes=64)
        x_scales = const.tile([P, E * TOKENS], U8, align_bytes=64)
        b1_t = const.tile([P, P], F32)

        def prepare_x_and_b1():
            x_t = psum_setup.tile([P, E, PACK, TOKENS], BF16)
            for e in range(E):
                for t in range(PACK):
                    nc.tensor.transpose(
                        x_t[:, e, t, :], x_rows[:, e, t * P : (t + 1) * P], identity[:]
                    )
            x_grouped = const.tile([P, E, TOKENS, PACK], BF16, align_bytes=64)
            nc.vector.tensor_copy(out=x_grouped[:], in_=x_t[:].rearrange("p e t n -> p e n t"))
            b1_t_psum = psum_setup.tile([P, P], BF16)
            nc.tensor.transpose(b1_t_psum[:], b1_rows[:], identity[:])
            nc.vector.tensor_copy(out=b1_t[:], in_=b1_t_psum[:])
            nc.vector.quantize_mx(
                out=x_words[:].bitcast(FP8X4),
                scales=x_scales[:],
                in_=x_grouped[:].rearrange("p e n t -> p (e n t)"),
            )

        b2_all = const.tile([P, E * D], BF16)
        b2_scaled = const.tile([P, E * D], F32)

        def first_matmul(j, w1_words, w1_scales):
            tokens = slice((j // EXPERT_UNITS) * TOKENS, (j // EXPERT_UNITS + 1) * TOKENS)
            product = []
            for q in range(UNIT_PASSES):
                bank = psum_hidden.tile([P, PACK, TOKENS], F32, name="bank")
                for t in range(PACK):
                    columns = slice((q * PACK + t) * P, (q * PACK + t + 1) * P)
                    nc.tensor.matmul_mx(
                        out=bank[:, t, :],
                        lhsT=w1_words[:, columns].bitcast(FP8X4),
                        lhsT_scale=w1_scales[:, columns],
                        rhs=x_words[:, tokens].bitcast(FP8X4),
                        rhs_scale=x_scales[:, tokens],
                        start=True,
                        stop=True,
                    )
                product.append(bank)
            return product

        def add_bias(j, product):
            biased = hidden_pool.tile([P, UNIT_PASSES, TOKENS, PACK], BF16, name="biased")
            for q in range(UNIT_PASSES):
                first = (j * UNIT_PASSES + q) * PACK
                nc.vector.tensor_tensor(
                    out=biased[:, q, :, :],
                    in0=product[q][:].rearrange("p t n -> p n t"),
                    in1=b1_t[:, first : first + PACK].unsqueeze(1).to_broadcast([P, TOKENS, PACK]),
                    op=ALU.add,
                )
            return biased

        def relu(biased):
            h = hidden_pool.tile([P, UNIT_PASSES * TOKENS * PACK], BF16, name="h", align_bytes=64)
            nc.vector.tensor_scalar_max(
                out=h[:], in0=biased[:].rearrange("p q n t -> p (q n t)"), scalar1=0.0
            )
            return h

        def quantise_hidden(h):
            h_words = hidden_pool.tile([P, UNIT_PASSES * TOKENS], U32, name="h_words", align_bytes=64)
            h_scales = hidden_pool.tile([P, UNIT_PASSES * TOKENS], U8, name="h_scales", align_bytes=64)
            nc.vector.quantize_mx(out=h_words[:].bitcast(FP8X4), scales=h_scales[:], in_=h[:])
            return h_words, h_scales

        def second_matmul(j, y, h_words, h_scales, w2_words, w2_scales):
            for q in range(UNIT_PASSES):
                g = (j % EXPERT_UNITS) * UNIT_PASSES + q
                nc.tensor.matmul_mx(
                    out=y[:],
                    lhsT=h_words[:, q * TOKENS : (q + 1) * TOKENS].bitcast(FP8X4),
                    lhsT_scale=h_scales[:, q * TOKENS : (q + 1) * TOKENS],
                    rhs=w2_words[:, q * D : (q + 1) * D].bitcast(FP8X4),
                    rhs_scale=w2_scales[:, q * D : (q + 1) * D],
                    start=(g == 0),
                    stop=(g == PASSES - 1),
                )

        def finish(e, y):
            result = hidden_pool.tile([P, D], F32, name="result")
            nc.vector.scalar_tensor_tensor(
                out=result[:],
                in0=y[:],
                scalar=logit_scale[:, 0:1],
                in1=b2_scaled[:, e * D : (e + 1) * D],
                op0=ALU.mult,
                op1=ALU.add,
            )
            nc.sync.dma_start(out=out[e * TOKENS : (e + 1) * TOKENS, :], in_=result[:])

        groupeds = {}
        products = {}
        biaseds = {}
        hs = {}
        h_operands = {}
        ys = {}
        for s in range(len(stream) + 2):
            if s + LOAD_AHEAD < len(stream):
                raws[s + LOAD_AHEAD] = load_unit(*stream[s + LOAD_AHEAD])
            if s < len(stream):
                groupeds[s] = regroup(raws[s])
            if s == 0:
                prepare_x_and_b1()
            if s == B2_LOAD_STEP:
                nc.sync.dma_start(
                    out=b2_all[:], in_=b2.rearrange("e d -> (e d)").partition_broadcast(P)
                )
            if s == B2_SCALE_STEP:
                nc.vector.tensor_scalar_mul(
                    out=b2_scaled[:], in0=b2_all[:], scalar1=logit_scale[:, 0:1]
                )

            weight, j = unit_at(s - 4)
            if weight == "W1":
                h_operands[j] = quantise_hidden(hs[j])

            weight, j = unit_at(s - 3)
            if weight == "W1":
                biaseds[j] = add_bias(j, products[j])

            weight, j = unit_at(s - 1)
            if weight == "W1":
                products[j] = first_matmul(j, *quantise(groupeds[s - 1]))
            if weight == "W2":
                if j % EXPERT_UNITS == 0:
                    ys[j // EXPERT_UNITS] = psum_y.tile([P, D], F32, name="y")
                second_matmul(j, ys[j // EXPERT_UNITS], *h_operands[j], *quantise(groupeds[s - 1]))

            weight, j = unit_at(s - 3)
            if weight == "W1":
                hs[j] = relu(biaseds[j])

            weight, j = unit_at(s - 2)
            if weight == "W2" and j % EXPERT_UNITS == EXPERT_UNITS - 1:
                finish(j // EXPERT_UNITS, ys[j // EXPERT_UNITS])
